import numpy as np
import ml_dtypes


def mxq(x, axis, fmt="e4m3"):
    dtype, down = {"e4m3": (ml_dtypes.float8_e4m3fn, 7), "e5m2": (ml_dtypes.float8_e5m2, 14)}[fmt]
    v = np.moveaxis(np.asarray(x, np.float32).astype(ml_dtypes.bfloat16).astype(np.float64), axis, -1)
    blocks = v.reshape(v.shape[:-1] + (-1, 32))
    amax = np.abs(blocks).max(-1, keepdims=True)
    byte = np.maximum(np.where(amax > 0, np.frexp(amax)[1] - 1 + 127, 0) - down, 1)
    scale = np.exp2(byte - 127.0)
    codes = (blocks / scale).astype(np.float32).astype(dtype).astype(np.float64)
    return np.moveaxis((codes * scale).reshape(v.shape), -1, axis)


WIDE = False


def mx_kscale(k):
    if not WIDE:
        return np.ones(k)
    levels = np.array([10, -10, 5, -5, 0])
    a = np.random.permutation(np.resize(levels, k // 512 * 4)).reshape(k // 512, 4)
    idx = np.arange(k)
    return np.exp2(a[idx // 512, idx % 128 // 32])


BF16 = ml_dtypes.bfloat16


def bf(x):
    return np.asarray(x, np.float32).astype(BF16)


def f64(x):
    return np.asarray(x).astype(np.float64)


B, S, I0, I1, I2, I3, I4, O0, O1, O2, O3, O4, R1, R2, R3, R4 = 2, 256, 4, 4, 2, 2, 16, 4, 8, 2, 2, 32, 16, 512, 1024, 512
IA, OA = I0 * I1, O0 * O1


def tt_step(t, c):
    I, O, r = t.shape
    _, i, o, q = c.shape
    p = mxq(t.reshape(I * O, r), 1, "e4m3") @ mxq(c.reshape(r, i * o * q), 0, "e4m3")
    return p.reshape(I, O, i, o, q).transpose(0, 2, 1, 3, 4).reshape(I * i, O * o, q)


def setup_inputs():
    s, u = mx_kscale(R2), mx_kscale(R3)
    return {"t1": bf(np.random.standard_normal((IA, OA, R2)) * s),
            "core2": bf(np.random.standard_normal((R2, I2, O2, R3)) / np.sqrt(R2) / s[:, None, None, None] * u),
            "core3": bf(np.random.standard_normal((R3, I3, O3, R4)) / np.sqrt(R3) / u[:, None, None, None])}


def reference(t1, core2, core3):
    t2 = tt_step(f64(t1), f64(core2))
    return tt_step(t2, f64(core3))

@@ -1,0 +1,197 @@
+from contextlib import ExitStack
+
+import concourse.bass as bass
+import concourse.mybir as mybir
+import concourse.tile as tile
+from concourse.masks import make_identity
+
+F32 = mybir.dt.float32
+BF16 = mybir.dt.bfloat16
+U32 = mybir.dt.uint32
+U8 = mybir.dt.uint8
+FP8X4 = mybir.dt.float8_e4m3fn_x4
+
+P = 128
+FLOPS = 2 * 512 * 512 * 4096 + 2 * 2048 * 1024 * 2048
+
+S_GROUPS = {"a0": 40, "b0": 40}
+
+
+def tile_linear2mpo_pa_kernel(tc, t1, core2, core3, out):
+    nc = tc.nc
+    t1v = t1.flatten_outer_dims().rearrange("(h p) r -> p h r", p=P)
+    c2v = core2.rearrange("(p j) i o q -> p j (i o) q", j=4)
+    c3v = core3.rearrange("(g t p) i o q -> p (g t) (i o) q", g=2, t=4)
+    outv = out.rearrange("(ib x i) (ob y o) q -> ib x y ob i (o q)", x=2, i=2, y=2, o=2)
+
+    with ExitStack() as ctx:
+        keep = ctx.enter_context(tc.tile_pool(name="keep", bufs=1))
+        rawp = ctx.enter_context(tc.tile_pool(name="rawp", bufs=8))
+        grpp = ctx.enter_context(tc.tile_pool(name="grpp", bufs=3))
+        t2gp = ctx.enter_context(tc.tile_pool(name="t2gp", bufs=4))
+        ostp = ctx.enter_context(tc.tile_pool(name="ostp", bufs=12))
+        psa = ctx.enter_context(tc.psum_pool(name="psa", bufs=3))
+        psb = ctx.enter_context(tc.psum_pool(name="psb", bufs=5))
+
+        t1_sb = keep.tile([P, 2048], BF16, name="t1_sb")
+        nc.sync.dma_start(out=t1_sb[:].rearrange("p (h r) -> p h r", h=4), in_=t1v)
+        raw = {}
+        for w in ("a0", "b0", "a1", "b1", "b2", "b3", "a2", "a3"):
+            n = int(w[1])
+            if w[0] == "a":
+                r = rawp.tile([P, 4, 1024], BF16, name="raw_" + w, tag="raw")
+                nc.sync.dma_start(out=r[:], in_=c2v[:, :, n, :])
+            else:
+                r = rawp.tile([P, 8, 512], BF16, name="raw_" + w, tag="raw")
+                nc.sync.dma_start(out=r[:], in_=c3v[:, :, n, :])
+            raw[w] = r
+
+        ident = keep.tile([P, P], F32, name="ident")
+        make_identity(nc, ident[:])
+
+        t1g = keep.tile([P, 2048], BF16, name="t1g", align_bytes=64)
+        t1c = keep.tile([P, 512], U32, name="t1c", align_bytes=64)
+        t1s = keep.tile([P, 512], U8, name="t1s", align_bytes=64)
+        c2c = keep.tile([P, 4, 1024], U32, name="c2c", align_bytes=64)
+        c2s = keep.tile([P, 4, 1024], U8, name="c2s", align_bytes=64)
+        c3c = keep.tile([P, 4, 1024], U32, name="c3c", align_bytes=64)
+        c3s = keep.tile([P, 4, 1024], U8, name="c3s", align_bytes=64)
+        t2c = keep.tile([P, 4, 4, 256], U32, name="t2c", align_bytes=64)
+        t2s = keep.tile([P, 4, 4, 256], U8, name="t2s", align_bytes=64)
+
+        def copy(eng, dst, src):
+            if eng == "S":
+                nc.scalar.copy(out=dst, in_=src)
+            else:
+                nc.vector.tensor_copy(out=dst, in_=src)
+
+        t1w = t1_sb[:].bitcast(F32).rearrange("p (h w u) -> p h u w", h=4, u=2)
+        t1gw = t1g[:].bitcast(F32).rearrange("p (h o l u) -> p h o l u", h=4, o=32, l=4, u=2)
+        for h in range(4):
+            pst = psa.tile([P, 2, P], F32, name="pst", tag="pa")
+            for u in range(2):
+                nc.tensor.transpose(pst[:, u, :], t1w[:, h, u, :], ident[:])
+            copy("VS"[h % 2], t1gw[:, h], pst[:].rearrange("p u (l o) -> p o l u", l=4))
+        nc.vector.quantize_mx(out=t1c[:].bitcast(FP8X4), scales=t1s[:], in_=t1g[:])
+
+        grouped = {}
+
+        def regroup(w):
+            g_t = grpp.tile([P, 4096], BF16, name="grp_" + w, tag="grp", align_bytes=64)
+            grouped[w] = g_t
+            cs = S_GROUPS.get(w, 0)
+            if w[0] == "a":
+                pieces = [(g_t[:, 2048 * z : 2048 * (z + 1)], raw[w][:, :, 512 * z : 512 * (z + 1)]) for z in range(2)]
+            else:
+                pieces = [(g_t[:, 2048 * z : 2048 * (z + 1)], raw[w][:, 4 * z : 4 * z + 4, :]) for z in range(2)]
+            for dst, src in pieces:
+                d = dst.rearrange("p (c i t) -> p c t i", i=4, t=4)
+                s = src.rearrange("p t (c i) -> p c t i", i=4)
+                if cs > 0:
+                    copy("S", d[:, 128 - cs :], s[:, 128 - cs :])
+                copy("V", d[:, : 128 - cs], s[:, : 128 - cs])
+
+        def quant(w):
+            n = int(w[1])
+            codes, scales = (c2c, c2s) if w[0] == "a" else (c3c, c3s)
+            nc.vector.quantize_mx(out=codes[:, n, :].bitcast(FP8X4), scales=scales[:, n, :], in_=grouped[w][:])
+
+        t2g = {}
+
+        def step_a(a, h):
+            tg = t2gp.tile([P, 2, P, 4], BF16, name="t2g", tag="t2g", align_bytes=64)
+            t2g[(a, h)] = tg
+            for g in range(2):
+                pa = psa.tile([P, 4, P], F32, name="pa", tag="pa")
+                for t in range(4):
+                    cols = slice((4 * g + t) * P, (4 * g + t + 1) * P)
+                    nc.tensor.matmul_mx(
+                        out=pa[:, t, :],
+                        lhsT=c2c[:, a, cols].bitcast(FP8X4),
+                        lhsT_scale=c2s[:, a, cols],
+                        rhs=t1c[:, h * P : (h + 1) * P].bitcast(FP8X4),
+                        rhs_scale=t1s[:, h * P : (h + 1) * P],
+                        start=True,
+                        stop=True,
+                    )
+                copy("S", tg[:, g], pa[:].rearrange("p t w -> p w t"))
+
+        def quant_t2(a, h):
+            nc.vector.quantize_mx(
+                out=t2c[:, a, h, :].bitcast(FP8X4),
+                scales=t2s[:, a, h, :],
+                in_=t2g[(a, h)][:].rearrange("p g w t -> p (g w t)"),
+            )
+
+        ost = {}
+
+        def step_b(a, h, b):
+            pb = psb.tile([P, 512], F32, name="pb", tag="pb")
+            for g in range(2):
+                nc.tensor.matmul_mx(
+                    out=pb[:],
+                    lhsT=t2c[:, a, h, g * P : (g + 1) * P].bitcast(FP8X4),
+                    lhsT_scale=t2s[:, a, h, g * P : (g + 1) * P],
+                    rhs=c3c[:, b, g * 512 : (g + 1) * 512].bitcast(FP8X4),
+                    rhs_scale=c3s[:, b, g * 512 : (g + 1) * 512],
+                    start=(g == 0),
+                    stop=(g == 1),
+                )
+            i, o = b // 2, b % 2
+            if o == 0:
+                ost[(a, h, i)] = ostp.tile([P, 1024], F32, name="ost", tag="ost")
+            os_t = ost[(a, h, i)]
+            copy("V" if (a >= 2 and o == 1) else "S", os_t[:, o * 512 : (o + 1) * 512], pb[:])
+            if o == 1:
+                for l in range(4):
+                    nc.sync.dma_start(out=outv[4 * h + l, a // 2, a % 2, :, i, :], in_=os_t[l:P:4, :])
+
+        H = range(4)
+        regroup("a0")
+        quant("a0")
+        regroup("b0")
+        for h in H:
+            step_a(0, h)
+        quant("b0")
+        for h in H:
+            quant_t2(0, h)
+        regroup("a1")
+        for h in H:
+            step_b(0, h, 0)
+        quant("a1")
+        regroup("b1")
+        for h in H:
+            step_a(1, h)
+        quant("b1")
+        for h in H:
+            quant_t2(1, h)
+        regroup("b2")
+        for h in H:
+            step_b(0, h, 1)
+        quant("b2")
+        regroup("b3")
+        for h in H:
+            step_b(1, h, 0)
+        for h in H:
+            step_b(1, h, 1)
+        quant("b3")
+        regroup("a2")
+        for h in H:
+            step_b(0, h, 2)
+            step_b(0, h, 3)
+        quant("a2")
+        regroup("a3")
+        for h in H:
+            step_a(2, h)
+            step_b(1, h, 2)
+            step_b(1, h, 3)
+            quant_t2(2, h)
+        quant("a3")
+        for h in H:
+            step_a(3, h)
+            for b in range(4):
+                step_b(2, h, b)
+            quant_t2(3, h)
+        for h in H:
+            for b in range(4):
+                step_b(3, h, b)

@@ -1,8 +1,6 @@
 from contextlib import ExitStack
 
-import concourse.bass as bass
 import concourse.mybir as mybir
-import concourse.tile as tile
 from concourse.masks import make_identity
 
 F32 = mybir.dt.float32
@@ -14,6 +12,7 @@ FP8X4 = mybir.dt.float8_e4m3fn_x4
 P = 128
 FLOPS = 2 * 512 * 512 * 4096 + 2 * 2048 * 1024 * 2048
 
+MANUAL = True
 S_GROUPS = {"a0": 40, "b0": 40}
 
 
@@ -22,29 +21,47 @@ def tile_linear2mpo_pa_kernel(tc, t1, core2, core3, out):
     t1v = t1.flatten_outer_dims().rearrange("(h p) r -> p h r", p=P)
     c2v = core2.rearrange("(p j) i o q -> p j (i o) q", j=4)
     c3v = core3.rearrange("(g t p) i o q -> p (g t) (i o) q", g=2, t=4)
-    outv = out.rearrange("(ib x i) (ob y o) q -> ib x y ob i (o q)", x=2, i=2, y=2, o=2)
+    out_y = out.rearrange("(ib x i) (ob y o) q -> ib x y ob i (o q)", x=2, i=2, y=2, o=2)
+    out_x = out.rearrange("(ib x i) (ob y o) q -> ib x i ob (y o q)", x=2, i=2, y=2, o=2)
 
     with ExitStack() as ctx:
         keep = ctx.enter_context(tc.tile_pool(name="keep", bufs=1))
-        rawp = ctx.enter_context(tc.tile_pool(name="rawp", bufs=8))
+        rawp = ctx.enter_context(tc.tile_pool(name="rawp", bufs=6))
         grpp = ctx.enter_context(tc.tile_pool(name="grpp", bufs=3))
         t2gp = ctx.enter_context(tc.tile_pool(name="t2gp", bufs=4))
-        ostp = ctx.enter_context(tc.tile_pool(name="ostp", bufs=12))
+        ostp = ctx.enter_context(tc.tile_pool(name="ostp", bufs=6))
         psa = ctx.enter_context(tc.psum_pool(name="psa", bufs=3))
         psb = ctx.enter_context(tc.psum_pool(name="psb", bufs=5))
+        if MANUAL:
+            ctx.enter_context(tc.manual_schedule())
 
         t1_sb = keep.tile([P, 2048], BF16, name="t1_sb")
         nc.sync.dma_start(out=t1_sb[:].rearrange("p (h r) -> p h r", h=4), in_=t1v)
         raw = {}
-        for w in ("a0", "b0", "a1", "b1", "b2", "b3", "a2", "a3"):
-            n = int(w[1])
-            if w[0] == "a":
-                r = rawp.tile([P, 4, 1024], BF16, name="raw_" + w, tag="raw")
-                nc.sync.dma_start(out=r[:], in_=c2v[:, :, n, :])
-            else:
-                r = rawp.tile([P, 8, 512], BF16, name="raw_" + w, tag="raw")
-                nc.sync.dma_start(out=r[:], in_=c3v[:, :, n, :])
-            raw[w] = r
+
+        def load_a(n):
+            r = rawp.tile([P, 4, 1024], BF16, name="raw_a", tag="raw")
+            nc.sync.dma_start(out=r[:], in_=c2v[:, :, n, :])
+            for z in range(2):
+                raw[("a%d" % n, z)] = r[:, :, 512 * z : 512 * (z + 1)]
+
+        def load_b(n):
+            r = rawp.tile([P, 8, 512], BF16, name="raw_b", tag="raw")
+            nc.sync.dma_start(out=r[:], in_=c3v[:, :, n, :])
+            for z in range(2):
+                raw[("b%d" % n, z)] = r[:, 4 * z : 4 * z + 4, :]
+
+        load_a(0)
+        load_b(0)
+        load_a(1)
+        load_b(1)
+        r23 = keep.tile([P, 8, 2, 512], BF16, name="r23")
+        nc.sync.dma_start(out=r23[:], in_=c3v[:, :, 2:4, :])
+        for n in range(2, 4):
+            for z in range(2):
+                raw[("b%d" % n, z)] = r23[:, 4 * z : 4 * z + 4, n - 2, :]
+        load_a(2)
+        load_a(3)
 
         ident = keep.tile([P, P], F32, name="ident")
         make_identity(nc, ident[:])
@@ -76,25 +93,31 @@ def tile_linear2mpo_pa_kernel(tc, t1, core2, core3, out):
 
         grouped = {}
 
-        def regroup(w):
-            g_t = grpp.tile([P, 4096], BF16, name="grp_" + w, tag="grp", align_bytes=64)
-            grouped[w] = g_t
-            cs = S_GROUPS.get(w, 0)
-            if w[0] == "a":
-                pieces = [(g_t[:, 2048 * z : 2048 * (z + 1)], raw[w][:, :, 512 * z : 512 * (z + 1)]) for z in range(2)]
-            else:
-                pieces = [(g_t[:, 2048 * z : 2048 * (z + 1)], raw[w][:, 4 * z : 4 * z + 4, :]) for z in range(2)]
-            for dst, src in pieces:
-                d = dst.rearrange("p (c i t) -> p c t i", i=4, t=4)
-                s = src.rearrange("p t (c i) -> p c t i", i=4)
-                if cs > 0:
-                    copy("S", d[:, 128 - cs :], s[:, 128 - cs :])
-                copy("V", d[:, : 128 - cs], s[:, : 128 - cs])
+        def views(w, z):
+            if w not in grouped:
+                grouped[w] = grpp.tile([P, 4096], BF16, name="grp", tag="grp", align_bytes=64)
+            d = grouped[w][:, 2048 * z : 2048 * (z + 1)].rearrange("p (c i t) -> p c t i", i=4, t=4)
+            s = raw[(w, z)].rearrange("p t (c i) -> p c t i", i=4)
+            return d, s, P - S_GROUPS.get(w, 0)
+
+        def regroup_s(w):
+            for z in range(2):
+                d, s, cv = views(w, z)
+                copy("S", d[:, cv:], s[:, cv:])
+
+        def regroup_v(w, z):
+            d, s, cv = views(w, z)
+            copy("V", d[:, :cv], s[:, :cv])
 
         def quant(w):
             n = int(w[1])
             codes, scales = (c2c, c2s) if w[0] == "a" else (c3c, c3s)
             nc.vector.quantize_mx(out=codes[:, n, :].bitcast(FP8X4), scales=scales[:, n, :], in_=grouped[w][:])
+
+        def prep(w):
+            regroup_v(w, 0)
+            regroup_v(w, 1)
+            quant(w)
 
         t2g = {}
 
@@ -114,7 +137,7 @@ def tile_linear2mpo_pa_kernel(tc, t1, core2, core3, out):
                         start=True,
                         stop=True,
                     )
-                copy("S", tg[:, g], pa[:].rearrange("p t w -> p w t"))
+                copy("V" if (a >= 2 and g == 1) else "S", tg[:, g], pa[:].rearrange("p t w -> p w t"))
 
         def quant_t2(a, h):
             nc.vector.quantize_mx(
@@ -138,55 +161,78 @@ def tile_linear2mpo_pa_kernel(tc, t1, core2, core3, out):
                     stop=(g == 1),
                 )
             i, o = b // 2, b % 2
-            if o == 0:
-                ost[(a, h, i)] = ostp.tile([P, 1024], F32, name="ost", tag="ost")
-            os_t = ost[(a, h, i)]
-            copy("V" if (a >= 2 and o == 1) else "S", os_t[:, o * 512 : (o + 1) * 512], pb[:])
-            if o == 1:
-                for l in range(4):
-                    nc.sync.dma_start(out=outv[4 * h + l, a // 2, a % 2, :, i, :], in_=os_t[l:P:4, :])
+            eng = "V" if (a >= 2 and o == 1) else "S"
+            if a < 2:
+                key = ("x", h, i)
+                if key not in ost:
+                    ost[key] = ostp.tile([P, 2, 2, 512], F32, name="ost", tag="ost")
+                os_t = ost[key]
+                copy(eng, os_t[:, a, o, :], pb[:])
+                if a == 1 and o == 1:
+                    for l in range(4):
+                        nc.sync.dma_start(
+                            out=out_x[4 * h + l, 0, i, :, :], in_=os_t[l:P:4].rearrange("p y o q -> p (y o q)")
+                        )
+            else:
+                key = ("y", a, h)
+                if key not in ost:
+                    ost[key] = ostp.tile([P, 2, 2, 512], F32, name="ost", tag="ost")
+                os_t = ost[key]
+                copy(eng, os_t[:, i, o, :], pb[:])
+                last = a == 3 and h == 3
+                if last and o == 1:
+                    for l in range(4):
+                        nc.sync.dma_start(
+                            out=out_y[4 * h + l, 1, a % 2, :, i, :], in_=os_t[l:P:4, i].rearrange("p o q -> p (o q)")
+                        )
+                elif b == 3:
+                    for l in range(4):
+                        nc.sync.dma_start(
+                            out=out_y[4 * h + l, 1, a % 2, :, :, :], in_=os_t[l:P:4].rearrange("p i o q -> p i (o q)")
+                        )
 
         H = range(4)
-        regroup("a0")
-        quant("a0")
-        regroup("b0")
+        regroup_s("a0")
+        prep("a0")
+        regroup_s("b0")
         for h in H:
             step_a(0, h)
-        quant("b0")
-        for h in H:
-            quant_t2(0, h)
-        regroup("a1")
+        prep("b0")
+        quant_t2(0, 0)
+        regroup_v("a1", 0)
+        quant_t2(0, 1)
+        regroup_v("a1", 1)
+        quant_t2(0, 2)
+        quant_t2(0, 3)
+        quant("a1")
         for h in H:
             step_b(0, h, 0)
-        quant("a1")
-        regroup("b1")
         for h in H:
             step_a(1, h)
-        quant("b1")
-        for h in H:
-            quant_t2(1, h)
-        regroup("b2")
-        for h in H:
-            step_b(0, h, 1)
+        prep("b1")
+        quant_t2(1, 0)
+        quant_t2(1, 1)
+        regroup_v("b2", 0)
+        quant_t2(1, 2)
+        quant_t2(1, 3)
+        regroup_v("b2", 1)
         quant("b2")
-        regroup("b3")
         for h in H:
             step_b(1, h, 0)
         for h in H:
+            step_b(0, h, 1)
             step_b(1, h, 1)
-        quant("b3")
-        regroup("a2")
+        prep("b3")
         for h in H:
             step_b(0, h, 2)
-            step_b(0, h, 3)
-        quant("a2")
-        regroup("a3")
+            step_b(1, h, 2)
+        prep("a2")
+        prep("a3")
         for h in H:
             step_a(2, h)
-            step_b(1, h, 2)
+            step_b(0, h, 3)
             step_b(1, h, 3)
             quant_t2(2, h)
-        quant("a3")
         for h in H:
             step_a(3, h)
             for b in range(4):

@@ -47,8 +47,8 @@ def tile_linear2mpo_pa_kernel(tc, t1, core2, core3, out):
 
         def load_b(n):
             r = rawp.tile([P, 8, 512], BF16, name="raw_b", tag="raw")
-            nc.sync.dma_start(out=r[:], in_=c3v[:, :, n, :])
             for z in range(2):
+                nc.sync.dma_start(out=r[:, 4 * z : 4 * z + 4, :], in_=c3v[:, 4 * z : 4 * z + 4, n, :])
                 raw[("b%d" % n, z)] = r[:, 4 * z : 4 * z + 4, :]
 
         load_a(0)
@@ -56,7 +56,8 @@ def tile_linear2mpo_pa_kernel(tc, t1, core2, core3, out):
         load_a(1)
         load_b(1)
         r23 = keep.tile([P, 8, 2, 512], BF16, name="r23")
-        nc.sync.dma_start(out=r23[:], in_=c3v[:, :, 2:4, :])
+        for z in range(2):
+            nc.sync.dma_start(out=r23[:, 4 * z : 4 * z + 4], in_=c3v[:, 4 * z : 4 * z + 4, 2:4, :])
         for n in range(2, 4):
             for z in range(2):
                 raw[("b%d" % n, z)] = r23[:, 4 * z : 4 * z + 4, n - 2, :]
@@ -112,7 +113,13 @@ def tile_linear2mpo_pa_kernel(tc, t1, core2, core3, out):
         def quant(w):
             n = int(w[1])
             codes, scales = (c2c, c2s) if w[0] == "a" else (c3c, c3s)
-            nc.vector.quantize_mx(out=codes[:, n, :].bitcast(FP8X4), scales=scales[:, n, :], in_=grouped[w][:])
+            for z in range(2):
+                cols = slice(512 * z, 512 * (z + 1))
+                nc.vector.quantize_mx(
+                    out=codes[:, n, cols].bitcast(FP8X4),
+                    scales=scales[:, n, cols],
+                    in_=grouped[w][:, 2048 * z : 2048 * (z + 1)],
+                )
 
         def prep(w):
             regroup_v(w, 0)

@@ -26,7 +26,7 @@ def tile_linear2mpo_pa_kernel(tc, t1, core2, core3, out):
 
     with ExitStack() as ctx:
         keep = ctx.enter_context(tc.tile_pool(name="keep", bufs=1))
-        rawp = ctx.enter_context(tc.tile_pool(name="rawp", bufs=6))
+        rawp = ctx.enter_context(tc.tile_pool(name="rawp", bufs=5))
         grpp = ctx.enter_context(tc.tile_pool(name="grpp", bufs=3))
         t2gp = ctx.enter_context(tc.tile_pool(name="t2gp", bufs=4))
         ostp = ctx.enter_context(tc.tile_pool(name="ostp", bufs=6))
@@ -36,14 +36,22 @@ def tile_linear2mpo_pa_kernel(tc, t1, core2, core3, out):
             ctx.enter_context(tc.manual_schedule())
 
         t1_sb = keep.tile([P, 2048], BF16, name="t1_sb")
-        nc.sync.dma_start(out=t1_sb[:].rearrange("p (h r) -> p h r", h=4), in_=t1v)
         raw = {}
 
         def load_a(n):
-            r = rawp.tile([P, 4, 1024], BF16, name="raw_a", tag="raw")
-            nc.sync.dma_start(out=r[:], in_=c2v[:, :, n, :])
-            for z in range(2):
-                raw[("a%d" % n, z)] = r[:, :, 512 * z : 512 * (z + 1)]
+            if n == 0:
+                r0 = keep.tile([P, 4, 512], BF16, name="raw_a0z0")
+                r1 = keep.tile([P, 4, 512], BF16, name="raw_a0z1")
+                nc.sync.dma_start(out=r0[:], in_=c2v[:, :, n, :512])
+                nc.sync.dma_start(out=t1_sb[:].rearrange("p (h r) -> p h r", h=4), in_=t1v)
+                nc.sync.dma_start(out=r1[:], in_=c2v[:, :, n, 512:])
+                raw[("a0", 0)] = r0[:]
+                raw[("a0", 1)] = r1[:]
+            else:
+                r = rawp.tile([P, 4, 1024], BF16, name="raw_a", tag="raw")
+                nc.sync.dma_start(out=r[:], in_=c2v[:, :, n, :])
+                for z in range(2):
+                    raw[("a%d" % n, z)] = r[:, :, 512 * z : 512 * (z + 1)]
 
         def load_b(n):
             r = rawp.tile([P, 8, 512], BF16, name="raw_b", tag="raw")
@@ -83,14 +91,6 @@ def tile_linear2mpo_pa_kernel(tc, t1, core2, core3, out):
             else:
                 nc.vector.tensor_copy(out=dst, in_=src)
 
-        t1w = t1_sb[:].bitcast(F32).rearrange("p (h w u) -> p h u w", h=4, u=2)
-        t1gw = t1g[:].bitcast(F32).rearrange("p (h o l u) -> p h o l u", h=4, o=32, l=4, u=2)
-        for h in range(4):
-            pst = psa.tile([P, 2, P], F32, name="pst", tag="pa")
-            for u in range(2):
-                nc.tensor.transpose(pst[:, u, :], t1w[:, h, u, :], ident[:])
-            copy("VS"[h % 2], t1gw[:, h], pst[:].rearrange("p u (l o) -> p o l u", l=4))
-        nc.vector.quantize_mx(out=t1c[:].bitcast(FP8X4), scales=t1s[:], in_=t1g[:])
 
         grouped = {}
 
@@ -101,25 +101,27 @@ def tile_linear2mpo_pa_kernel(tc, t1, core2, core3, out):
             s = raw[(w, z)].rearrange("p t (c i) -> p c t i", i=4)
             return d, s, P - S_GROUPS.get(w, 0)
 
-        def regroup_s(w):
-            for z in range(2):
-                d, s, cv = views(w, z)
-                copy("S", d[:, cv:], s[:, cv:])
+        def regroup_s(w, z):
+            d, s, cv = views(w, z)
+            copy("S", d[:, cv:], s[:, cv:])
 
         def regroup_v(w, z):
             d, s, cv = views(w, z)
             copy("V", d[:, :cv], s[:, :cv])
 
-        def quant(w):
+        def quant_half(w, z):
             n = int(w[1])
             codes, scales = (c2c, c2s) if w[0] == "a" else (c3c, c3s)
-            for z in range(2):
-                cols = slice(512 * z, 512 * (z + 1))
-                nc.vector.quantize_mx(
-                    out=codes[:, n, cols].bitcast(FP8X4),
-                    scales=scales[:, n, cols],
-                    in_=grouped[w][:, 2048 * z : 2048 * (z + 1)],
-                )
+            cols = slice(512 * z, 512 * (z + 1))
+            nc.vector.quantize_mx(
+                out=codes[:, n, cols].bitcast(FP8X4),
+                scales=scales[:, n, cols],
+                in_=grouped[w][:, 2048 * z : 2048 * (z + 1)],
+            )
+
+        def quant(w):
+            quant_half(w, 0)
+            quant_half(w, 1)
 
         def prep(w):
             regroup_v(w, 0)
@@ -199,9 +201,22 @@ def tile_linear2mpo_pa_kernel(tc, t1, core2, core3, out):
                         )
 
         H = range(4)
-        regroup_s("a0")
-        prep("a0")
-        regroup_s("b0")
+        regroup_s("a0", 0)
+        regroup_v("a0", 0)
+        quant_half("a0", 0)
+        t1w = t1_sb[:].bitcast(F32).rearrange("p (h w u) -> p h u w", h=4, u=2)
+        t1gw = t1g[:].bitcast(F32).rearrange("p (h o l u) -> p h o l u", h=4, o=32, l=4, u=2)
+        for h in H:
+            pst = psa.tile([P, 2, P], F32, name="pst", tag="pa")
+            for u in range(2):
+                nc.tensor.transpose(pst[:, u, :], t1w[:, h, u, :], ident[:])
+            copy("S", t1gw[:, h], pst[:].rearrange("p u (l o) -> p o l u", l=4))
+        regroup_s("a0", 1)
+        regroup_v("a0", 1)
+        nc.vector.quantize_mx(out=t1c[:].bitcast(FP8X4), scales=t1s[:], in_=t1g[:])
+        quant_half("a0", 1)
+        regroup_s("b0", 0)
+        regroup_s("b0", 1)
         for h in H:
             step_a(0, h)
         prep("b0")
@@ -236,14 +251,14 @@ def tile_linear2mpo_pa_kernel(tc, t1, core2, core3, out):
         prep("a2")
         prep("a3")
         for h in H:
-            step_a(2, h)
             step_b(0, h, 3)
             step_b(1, h, 3)
+            step_a(2, h)
             quant_t2(2, h)
         for h in H:
-            step_a(3, h)
             for b in range(4):
                 step_b(2, h, b)
+            step_a(3, h)
             quant_t2(3, h)
         for h in H:
             for b in range(4):

@@ -10,256 +10,264 @@ U8 = mybir.dt.uint8
 FP8X4 = mybir.dt.float8_e4m3fn_x4
 
 P = 128
+PACK = 4
+K_PASS = P * PACK
+N_TILES = 4
+N_QUARTERS = 4
+HALF = 512
+GROUPS = HALF // 4
+
 FLOPS = 2 * 512 * 512 * 4096 + 2 * 2048 * 1024 * 2048
 
-MANUAL = True
-S_GROUPS = {"a0": 40, "b0": 40}
+SCALAR_GROUPS = {(2, 0): 40, (3, 0): 56}
 
 
 def tile_linear2mpo_pa_kernel(tc, t1, core2, core3, out):
     nc = tc.nc
-    t1v = t1.flatten_outer_dims().rearrange("(h p) r -> p h r", p=P)
-    c2v = core2.rearrange("(p j) i o q -> p j (i o) q", j=4)
-    c3v = core3.rearrange("(g t p) i o q -> p (g t) (i o) q", g=2, t=4)
-    out_y = out.rearrange("(ib x i) (ob y o) q -> ib x y ob i (o q)", x=2, i=2, y=2, o=2)
-    out_x = out.rearrange("(ib x i) (ob y o) q -> ib x i ob (y o q)", x=2, i=2, y=2, o=2)
+    t1_view = t1.flatten_outer_dims().rearrange("(h p) r -> p h r", p=P)
+    core2_view = core2.rearrange("(p j) i o q -> p j (i o) q", j=PACK)
+    core3_view = core3.rearrange("(g t p) i o q -> p (g t) (i o) q", g=2, t=PACK)
+    out_by_i = out.rearrange("(ib x i) (ob y o) q -> ib x y ob i (o q)", x=2, i=2, y=2, o=2)
+    out_by_o1 = out.rearrange("(ib x i) (ob y o) q -> ib x i ob (y o q)", x=2, i=2, y=2, o=2)
 
     with ExitStack() as ctx:
         keep = ctx.enter_context(tc.tile_pool(name="keep", bufs=1))
-        rawp = ctx.enter_context(tc.tile_pool(name="rawp", bufs=5))
-        grpp = ctx.enter_context(tc.tile_pool(name="grpp", bufs=3))
-        t2gp = ctx.enter_context(tc.tile_pool(name="t2gp", bufs=4))
-        ostp = ctx.enter_context(tc.tile_pool(name="ostp", bufs=6))
-        psa = ctx.enter_context(tc.psum_pool(name="psa", bufs=3))
-        psb = ctx.enter_context(tc.psum_pool(name="psb", bufs=5))
-        if MANUAL:
-            ctx.enter_context(tc.manual_schedule())
+        raw_pool = ctx.enter_context(tc.tile_pool(name="raw", bufs=5))
+        grouped_pool = ctx.enter_context(tc.tile_pool(name="grouped", bufs=3))
+        t2_pool = ctx.enter_context(tc.tile_pool(name="t2", bufs=N_TILES))
+        stage_pool = ctx.enter_context(tc.tile_pool(name="stage", bufs=6))
+        psum1 = ctx.enter_context(tc.psum_pool(name="psum1", bufs=3))
+        psum2 = ctx.enter_context(tc.psum_pool(name="psum2", bufs=5))
+        ctx.enter_context(tc.manual_schedule())
 
-        t1_sb = keep.tile([P, 2048], BF16, name="t1_sb")
         raw = {}
+        t1_rows = keep.tile([P, N_TILES * K_PASS], BF16, name="t1_rows")
 
-        def load_a(n):
-            if n == 0:
-                r0 = keep.tile([P, 4, 512], BF16, name="raw_a0z0")
-                r1 = keep.tile([P, 4, 512], BF16, name="raw_a0z1")
-                nc.sync.dma_start(out=r0[:], in_=c2v[:, :, n, :512])
-                nc.sync.dma_start(out=t1_sb[:].rearrange("p (h r) -> p h r", h=4), in_=t1v)
-                nc.sync.dma_start(out=r1[:], in_=c2v[:, :, n, 512:])
-                raw[("a0", 0)] = r0[:]
-                raw[("a0", 1)] = r1[:]
-            else:
-                r = rawp.tile([P, 4, 1024], BF16, name="raw_a", tag="raw")
-                nc.sync.dma_start(out=r[:], in_=c2v[:, :, n, :])
-                for z in range(2):
-                    raw[("a%d" % n, z)] = r[:, :, 512 * z : 512 * (z + 1)]
-
-        def load_b(n):
-            r = rawp.tile([P, 8, 512], BF16, name="raw_b", tag="raw")
+        def load_core2_quarter(a):
+            tile_a = raw_pool.tile([P, PACK, 2 * HALF], BF16, name="raw2", tag="raw")
+            nc.sync.dma_start(out=tile_a[:], in_=core2_view[:, :, a, :])
             for z in range(2):
-                nc.sync.dma_start(out=r[:, 4 * z : 4 * z + 4, :], in_=c3v[:, 4 * z : 4 * z + 4, n, :])
-                raw[("b%d" % n, z)] = r[:, 4 * z : 4 * z + 4, :]
+                raw[(2, a, z)] = tile_a[:, :, HALF * z : HALF * (z + 1)]
 
-        load_a(0)
-        load_b(0)
-        load_a(1)
-        load_b(1)
-        r23 = keep.tile([P, 8, 2, 512], BF16, name="r23")
+        def load_core3_quarter(b):
+            tile_b = raw_pool.tile([P, 2 * PACK, HALF], BF16, name="raw3", tag="raw")
+            for z in range(2):
+                rows = slice(PACK * z, PACK * (z + 1))
+                nc.sync.dma_start(out=tile_b[:, rows, :], in_=core3_view[:, rows, b, :])
+                raw[(3, b, z)] = tile_b[:, rows, :]
+
+        first_halves = [keep.tile([P, PACK, HALF], BF16, name="raw2_first%d" % z) for z in range(2)]
+        nc.sync.dma_start(out=first_halves[0][:], in_=core2_view[:, :, 0, :HALF])
+        nc.sync.dma_start(out=t1_rows[:].rearrange("p (h r) -> p h r", h=N_TILES), in_=t1_view)
+        nc.sync.dma_start(out=first_halves[1][:], in_=core2_view[:, :, 0, HALF:])
         for z in range(2):
-            nc.sync.dma_start(out=r23[:, 4 * z : 4 * z + 4], in_=c3v[:, 4 * z : 4 * z + 4, 2:4, :])
-        for n in range(2, 4):
-            for z in range(2):
-                raw[("b%d" % n, z)] = r23[:, 4 * z : 4 * z + 4, n - 2, :]
-        load_a(2)
-        load_a(3)
+            raw[(2, 0, z)] = first_halves[z][:]
+        load_core3_quarter(0)
+        load_core2_quarter(1)
+        load_core3_quarter(1)
+        raw3_last = keep.tile([P, 2 * PACK, 2, HALF], BF16, name="raw3_last")
+        for z in range(2):
+            rows = slice(PACK * z, PACK * (z + 1))
+            nc.sync.dma_start(out=raw3_last[:, rows], in_=core3_view[:, rows, 2:4, :])
+            for b in (2, 3):
+                raw[(3, b, z)] = raw3_last[:, rows, b - 2, :]
+        load_core2_quarter(2)
+        load_core2_quarter(3)
 
-        ident = keep.tile([P, P], F32, name="ident")
-        make_identity(nc, ident[:])
+        identity = keep.tile([P, P], F32, name="identity")
+        make_identity(nc, identity[:])
 
-        t1g = keep.tile([P, 2048], BF16, name="t1g", align_bytes=64)
-        t1c = keep.tile([P, 512], U32, name="t1c", align_bytes=64)
-        t1s = keep.tile([P, 512], U8, name="t1s", align_bytes=64)
-        c2c = keep.tile([P, 4, 1024], U32, name="c2c", align_bytes=64)
-        c2s = keep.tile([P, 4, 1024], U8, name="c2s", align_bytes=64)
-        c3c = keep.tile([P, 4, 1024], U32, name="c3c", align_bytes=64)
-        c3s = keep.tile([P, 4, 1024], U8, name="c3s", align_bytes=64)
-        t2c = keep.tile([P, 4, 4, 256], U32, name="t2c", align_bytes=64)
-        t2s = keep.tile([P, 4, 4, 256], U8, name="t2s", align_bytes=64)
+        t1_grouped = keep.tile([P, N_TILES * K_PASS], BF16, name="t1_grouped", align_bytes=64)
+        t1_codes = keep.tile([P, N_TILES * P], U32, name="t1_codes", align_bytes=64)
+        t1_scales = keep.tile([P, N_TILES * P], U8, name="t1_scales", align_bytes=64)
+        codes = {}
+        scales = {}
+        for core in (2, 3):
+            codes[core] = keep.tile([P, N_QUARTERS, 2 * HALF], U32, name="codes%d" % core, align_bytes=64)
+            scales[core] = keep.tile([P, N_QUARTERS, 2 * HALF], U8, name="scales%d" % core, align_bytes=64)
+        t2_codes = keep.tile([P, N_QUARTERS, N_TILES, 2 * P], U32, name="t2_codes", align_bytes=64)
+        t2_scales = keep.tile([P, N_QUARTERS, N_TILES, 2 * P], U8, name="t2_scales", align_bytes=64)
 
-        def copy(eng, dst, src):
-            if eng == "S":
+        def copy(engine, dst, src):
+            if engine == "scalar":
                 nc.scalar.copy(out=dst, in_=src)
             else:
                 nc.vector.tensor_copy(out=dst, in_=src)
 
-
         grouped = {}
 
-        def views(w, z):
-            if w not in grouped:
-                grouped[w] = grpp.tile([P, 4096], BF16, name="grp", tag="grp", align_bytes=64)
-            d = grouped[w][:, 2048 * z : 2048 * (z + 1)].rearrange("p (c i t) -> p c t i", i=4, t=4)
-            s = raw[(w, z)].rearrange("p t (c i) -> p c t i", i=4)
-            return d, s, P - S_GROUPS.get(w, 0)
+        def regroup(engine, core, n, z):
+            if (core, n) not in grouped:
+                grouped[(core, n)] = grouped_pool.tile([P, 2 * HALF * PACK], BF16, name="grouped", align_bytes=64)
+            half = grouped[(core, n)][:, HALF * PACK * z : HALF * PACK * (z + 1)]
+            dst = half.rearrange("p (c i t) -> p c t i", i=4, t=PACK)
+            src = raw[(core, n, z)].rearrange("p t (c i) -> p c t i", i=4)
+            split = GROUPS - SCALAR_GROUPS.get((core, n), 0)
+            if engine == "scalar":
+                copy(engine, dst[:, split:], src[:, split:])
+            else:
+                copy(engine, dst[:, :split], src[:, :split])
 
-        def regroup_s(w, z):
-            d, s, cv = views(w, z)
-            copy("S", d[:, cv:], s[:, cv:])
-
-        def regroup_v(w, z):
-            d, s, cv = views(w, z)
-            copy("V", d[:, :cv], s[:, :cv])
-
-        def quant_half(w, z):
-            n = int(w[1])
-            codes, scales = (c2c, c2s) if w[0] == "a" else (c3c, c3s)
-            cols = slice(512 * z, 512 * (z + 1))
+        def quantise(core, n, z):
+            words = slice(HALF * z, HALF * (z + 1))
             nc.vector.quantize_mx(
-                out=codes[:, n, cols].bitcast(FP8X4),
-                scales=scales[:, n, cols],
-                in_=grouped[w][:, 2048 * z : 2048 * (z + 1)],
+                out=codes[core][:, n, words].bitcast(FP8X4),
+                scales=scales[core][:, n, words],
+                in_=grouped[(core, n)][:, HALF * PACK * z : HALF * PACK * (z + 1)],
             )
 
-        def quant(w):
-            quant_half(w, 0)
-            quant_half(w, 1)
+        def quantise_both(core, n):
+            quantise(core, n, 0)
+            quantise(core, n, 1)
 
-        def prep(w):
-            regroup_v(w, 0)
-            regroup_v(w, 1)
-            quant(w)
+        def prepare(core, n):
+            regroup("vector", core, n, 0)
+            regroup("vector", core, n, 1)
+            quantise_both(core, n)
 
-        t2g = {}
+        t2_grouped = {}
 
-        def step_a(a, h):
-            tg = t2gp.tile([P, 2, P, 4], BF16, name="t2g", tag="t2g", align_bytes=64)
-            t2g[(a, h)] = tg
+        def step1(a, h):
+            t2_grouped[(a, h)] = t2_pool.tile([P, 2, P, PACK], BF16, name="t2_grouped", align_bytes=64)
+            rows = slice(h * P, (h + 1) * P)
             for g in range(2):
-                pa = psa.tile([P, 4, P], F32, name="pa", tag="pa")
-                for t in range(4):
-                    cols = slice((4 * g + t) * P, (4 * g + t + 1) * P)
+                bank = psum1.tile([P, PACK, P], F32, name="bank1", tag="bank1")
+                for t in range(PACK):
+                    cols = slice((PACK * g + t) * P, (PACK * g + t + 1) * P)
                     nc.tensor.matmul_mx(
-                        out=pa[:, t, :],
-                        lhsT=c2c[:, a, cols].bitcast(FP8X4),
-                        lhsT_scale=c2s[:, a, cols],
-                        rhs=t1c[:, h * P : (h + 1) * P].bitcast(FP8X4),
-                        rhs_scale=t1s[:, h * P : (h + 1) * P],
+                        out=bank[:, t, :],
+                        lhsT=codes[2][:, a, cols].bitcast(FP8X4),
+                        lhsT_scale=scales[2][:, a, cols],
+                        rhs=t1_codes[:, rows].bitcast(FP8X4),
+                        rhs_scale=t1_scales[:, rows],
                         start=True,
                         stop=True,
                     )
-                copy("V" if (a >= 2 and g == 1) else "S", tg[:, g], pa[:].rearrange("p t w -> p w t"))
+                engine = "vector" if (a >= 2 and g == 1) else "scalar"
+                copy(engine, t2_grouped[(a, h)][:, g], bank[:].rearrange("p t w -> p w t"))
 
-        def quant_t2(a, h):
+        def quantise_t2(a, h):
             nc.vector.quantize_mx(
-                out=t2c[:, a, h, :].bitcast(FP8X4),
-                scales=t2s[:, a, h, :],
-                in_=t2g[(a, h)][:].rearrange("p g w t -> p (g w t)"),
+                out=t2_codes[:, a, h, :].bitcast(FP8X4),
+                scales=t2_scales[:, a, h, :],
+                in_=t2_grouped[(a, h)][:].rearrange("p g w t -> p (g w t)"),
             )
 
-        ost = {}
+        stage = {}
 
-        def step_b(a, h, b):
-            pb = psb.tile([P, 512], F32, name="pb", tag="pb")
+        def store(dst_of_l, src_of_l):
+            for l in range(4):
+                nc.sync.dma_start(out=dst_of_l(l), in_=src_of_l(l))
+
+        def step2(a, h, b):
+            bank = psum2.tile([P, HALF], F32, name="bank2", tag="bank2")
             for g in range(2):
                 nc.tensor.matmul_mx(
-                    out=pb[:],
-                    lhsT=t2c[:, a, h, g * P : (g + 1) * P].bitcast(FP8X4),
-                    lhsT_scale=t2s[:, a, h, g * P : (g + 1) * P],
-                    rhs=c3c[:, b, g * 512 : (g + 1) * 512].bitcast(FP8X4),
-                    rhs_scale=c3s[:, b, g * 512 : (g + 1) * 512],
+                    out=bank[:],
+                    lhsT=t2_codes[:, a, h, g * P : (g + 1) * P].bitcast(FP8X4),
+                    lhsT_scale=t2_scales[:, a, h, g * P : (g + 1) * P],
+                    rhs=codes[3][:, b, g * HALF : (g + 1) * HALF].bitcast(FP8X4),
+                    rhs_scale=scales[3][:, b, g * HALF : (g + 1) * HALF],
                     start=(g == 0),
                     stop=(g == 1),
                 )
             i, o = b // 2, b % 2
-            eng = "V" if (a >= 2 and o == 1) else "S"
+            i1, o1 = a // 2, a % 2
+            engine = "vector" if (a >= 2 and o == 1) else "scalar"
             if a < 2:
-                key = ("x", h, i)
-                if key not in ost:
-                    ost[key] = ostp.tile([P, 2, 2, 512], F32, name="ost", tag="ost")
-                os_t = ost[key]
-                copy(eng, os_t[:, a, o, :], pb[:])
-                if a == 1 and o == 1:
-                    for l in range(4):
-                        nc.sync.dma_start(
-                            out=out_x[4 * h + l, 0, i, :, :], in_=os_t[l:P:4].rearrange("p y o q -> p (y o q)")
-                        )
+                key = ("both o1", h, i)
+                if key not in stage:
+                    stage[key] = stage_pool.tile([P, 2, 2, HALF], F32, name="stage", tag="stage")
+                tile_s = stage[key]
+                copy(engine, tile_s[:, o1, o, :], bank[:])
+                if o1 == 1 and o == 1:
+                    store(
+                        lambda l: out_by_o1[4 * h + l, i1, i, :, :],
+                        lambda l: tile_s[l:P:4].rearrange("p y o q -> p (y o q)"),
+                    )
             else:
-                key = ("y", a, h)
-                if key not in ost:
-                    ost[key] = ostp.tile([P, 2, 2, 512], F32, name="ost", tag="ost")
-                os_t = ost[key]
-                copy(eng, os_t[:, i, o, :], pb[:])
-                last = a == 3 and h == 3
-                if last and o == 1:
-                    for l in range(4):
-                        nc.sync.dma_start(
-                            out=out_y[4 * h + l, 1, a % 2, :, i, :], in_=os_t[l:P:4, i].rearrange("p o q -> p (o q)")
-                        )
-                elif b == 3:
-                    for l in range(4):
-                        nc.sync.dma_start(
-                            out=out_y[4 * h + l, 1, a % 2, :, :, :], in_=os_t[l:P:4].rearrange("p i o q -> p i (o q)")
-                        )
+                key = ("both i", a, h)
+                if key not in stage:
+                    stage[key] = stage_pool.tile([P, 2, 2, HALF], F32, name="stage", tag="stage")
+                tile_s = stage[key]
+                copy(engine, tile_s[:, i, o, :], bank[:])
+                very_last = a == N_QUARTERS - 1 and h == N_TILES - 1
+                if very_last and o == 1:
+                    store(
+                        lambda l: out_by_i[4 * h + l, i1, o1, :, i, :],
+                        lambda l: tile_s[l:P:4, i].rearrange("p o q -> p (o q)"),
+                    )
+                elif b == N_QUARTERS - 1:
+                    store(
+                        lambda l: out_by_i[4 * h + l, i1, o1, :, :, :],
+                        lambda l: tile_s[l:P:4].rearrange("p i o q -> p i (o q)"),
+                    )
 
-        H = range(4)
-        regroup_s("a0", 0)
-        regroup_v("a0", 0)
-        quant_half("a0", 0)
-        t1w = t1_sb[:].bitcast(F32).rearrange("p (h w u) -> p h u w", h=4, u=2)
-        t1gw = t1g[:].bitcast(F32).rearrange("p (h o l u) -> p h o l u", h=4, o=32, l=4, u=2)
-        for h in H:
-            pst = psa.tile([P, 2, P], F32, name="pst", tag="pa")
+        tiles = range(N_TILES)
+
+        regroup("scalar", 2, 0, 0)
+        regroup("vector", 2, 0, 0)
+        quantise(2, 0, 0)
+
+        t1_words = t1_rows[:].bitcast(F32).rearrange("p (h w u) -> p h u w", h=N_TILES, u=2)
+        t1_grouped_words = t1_grouped[:].bitcast(F32).rearrange("p (h o l u) -> p h o l u", h=N_TILES, o=32, l=4, u=2)
+        for h in tiles:
+            planes = psum1.tile([P, 2, P], F32, name="planes", tag="bank1")
             for u in range(2):
-                nc.tensor.transpose(pst[:, u, :], t1w[:, h, u, :], ident[:])
-            copy("S", t1gw[:, h], pst[:].rearrange("p u (l o) -> p o l u", l=4))
-        regroup_s("a0", 1)
-        regroup_v("a0", 1)
-        nc.vector.quantize_mx(out=t1c[:].bitcast(FP8X4), scales=t1s[:], in_=t1g[:])
-        quant_half("a0", 1)
-        regroup_s("b0", 0)
-        regroup_s("b0", 1)
-        for h in H:
-            step_a(0, h)
-        prep("b0")
-        quant_t2(0, 0)
-        regroup_v("a1", 0)
-        quant_t2(0, 1)
-        regroup_v("a1", 1)
-        quant_t2(0, 2)
-        quant_t2(0, 3)
-        quant("a1")
-        for h in H:
-            step_b(0, h, 0)
-        for h in H:
-            step_a(1, h)
-        prep("b1")
-        quant_t2(1, 0)
-        quant_t2(1, 1)
-        regroup_v("b2", 0)
-        quant_t2(1, 2)
-        quant_t2(1, 3)
-        regroup_v("b2", 1)
-        quant("b2")
-        for h in H:
-            step_b(1, h, 0)
-        for h in H:
-            step_b(0, h, 1)
-            step_b(1, h, 1)
-        prep("b3")
-        for h in H:
-            step_b(0, h, 2)
-            step_b(1, h, 2)
-        prep("a2")
-        prep("a3")
-        for h in H:
-            step_b(0, h, 3)
-            step_b(1, h, 3)
-            step_a(2, h)
-            quant_t2(2, h)
-        for h in H:
-            for b in range(4):
-                step_b(2, h, b)
-            step_a(3, h)
-            quant_t2(3, h)
-        for h in H:
-            for b in range(4):
-                step_b(3, h, b)
+                nc.tensor.transpose(planes[:, u, :], t1_words[:, h, u, :], identity[:])
+            copy("scalar", t1_grouped_words[:, h], planes[:].rearrange("p u (l o) -> p o l u", l=4))
+
+        regroup("scalar", 2, 0, 1)
+        regroup("vector", 2, 0, 1)
+        nc.vector.quantize_mx(out=t1_codes[:].bitcast(FP8X4), scales=t1_scales[:], in_=t1_grouped[:])
+        quantise(2, 0, 1)
+        regroup("scalar", 3, 0, 0)
+        regroup("scalar", 3, 0, 1)
+
+        for h in tiles:
+            step1(0, h)
+        prepare(3, 0)
+        quantise_t2(0, 0)
+        regroup("vector", 2, 1, 0)
+        quantise_t2(0, 1)
+        regroup("vector", 2, 1, 1)
+        quantise_t2(0, 2)
+        quantise_t2(0, 3)
+        quantise_both(2, 1)
+        for h in tiles:
+            step2(0, h, 0)
+
+        for h in tiles:
+            step1(1, h)
+        prepare(3, 1)
+        quantise_t2(1, 0)
+        quantise_t2(1, 1)
+        regroup("vector", 3, 2, 0)
+        quantise_t2(1, 2)
+        quantise_t2(1, 3)
+        regroup("vector", 3, 2, 1)
+        quantise_both(3, 2)
+        for h in tiles:
+            step2(1, h, 0)
+
+        for h in tiles:
+            step2(0, h, 1)
+            step2(1, h, 1)
+        prepare(3, 3)
+        for h in tiles:
+            step2(0, h, 2)
+            step2(1, h, 2)
+        prepare(2, 2)
+        prepare(2, 3)
+        for h in tiles:
+            step2(0, h, 3)
+            step2(1, h, 3)
+            step1(2, h)
+            quantise_t2(2, h)
+        for a in (2, 3):
+            for h in tiles:
+                for b in range(N_QUARTERS):
+                    step2(a, h, b)
+                if a == 2:
+                    step1(3, h)
+                    quantise_t2(3, h)

@@ -143,7 +143,7 @@ def tile_linear2mpo_pa_kernel(tc, t1, core2, core3, out):
                         start=True,
                         stop=True,
                     )
-                engine = "vector" if (a >= 2 and g == 1) else "scalar"
+                engine = "vector" if (a == 2 and g == 1) else "scalar"
                 copy(engine, t2_grouped[(a, h)][:, g], bank[:].rearrange("p t w -> p w t"))
 
         def quantise_t2(a, h):
@@ -264,10 +264,13 @@ def tile_linear2mpo_pa_kernel(tc, t1, core2, core3, out):
             step2(1, h, 3)
             step1(2, h)
             quantise_t2(2, h)
+        copied = []
         for a in (2, 3):
             for h in tiles:
                 for b in range(N_QUARTERS):
                     step2(a, h, b)
+                    if b == 1 and copied:
+                        quantise_t2(3, copied.pop())
                 if a == 2:
                     step1(3, h)
-                    quantise_t2(3, h)
+                    copied.append(h)

from contextlib import ExitStack

import concourse.mybir as mybir
from concourse.masks import make_identity

F32 = mybir.dt.float32
BF16 = mybir.dt.bfloat16
U32 = mybir.dt.uint32
U8 = mybir.dt.uint8
FP8X4 = mybir.dt.float8_e4m3fn_x4

P = 128
PACK = 4
K_PASS = P * PACK
N_TILES = 4
N_QUARTERS = 4
HALF = 512
GROUPS = HALF // 4

FLOPS = 2 * 512 * 512 * 4096 + 2 * 2048 * 1024 * 2048

SCALAR_GROUPS = {(2, 0): 40, (3, 0): 56}


def tile_linear2mpo_pa_kernel(tc, t1, core2, core3, out):
    nc = tc.nc
    t1_view = t1.flatten_outer_dims().rearrange("(h p) r -> p h r", p=P)
    core2_view = core2.rearrange("(p j) i o q -> p j (i o) q", j=PACK)
    core3_view = core3.rearrange("(g t p) i o q -> p (g t) (i o) q", g=2, t=PACK)
    out_by_i = out.rearrange("(ib x i) (ob y o) q -> ib x y ob i (o q)", x=2, i=2, y=2, o=2)
    out_by_o1 = out.rearrange("(ib x i) (ob y o) q -> ib x i ob (y o q)", x=2, i=2, y=2, o=2)

    with ExitStack() as ctx:
        keep = ctx.enter_context(tc.tile_pool(name="keep", bufs=1))
        raw_pool = ctx.enter_context(tc.tile_pool(name="raw", bufs=5))
        grouped_pool = ctx.enter_context(tc.tile_pool(name="grouped", bufs=3))
        t2_pool = ctx.enter_context(tc.tile_pool(name="t2", bufs=N_TILES))
        stage_pool = ctx.enter_context(tc.tile_pool(name="stage", bufs=6))
        psum1 = ctx.enter_context(tc.psum_pool(name="psum1", bufs=3))
        psum2 = ctx.enter_context(tc.psum_pool(name="psum2", bufs=5))
        ctx.enter_context(tc.manual_schedule())

        raw = {}
        t1_rows = keep.tile([P, N_TILES * K_PASS], BF16, name="t1_rows")

        def load_core2_quarter(a):
            tile_a = raw_pool.tile([P, PACK, 2 * HALF], BF16, name="raw2", tag="raw")
            nc.sync.dma_start(out=tile_a[:], in_=core2_view[:, :, a, :])
            for z in range(2):
                raw[(2, a, z)] = tile_a[:, :, HALF * z : HALF * (z + 1)]

        def load_core3_quarter(b):
            tile_b = raw_pool.tile([P, 2 * PACK, HALF], BF16, name="raw3", tag="raw")
            for z in range(2):
                rows = slice(PACK * z, PACK * (z + 1))
                nc.sync.dma_start(out=tile_b[:, rows, :], in_=core3_view[:, rows, b, :])
                raw[(3, b, z)] = tile_b[:, rows, :]

        first_halves = [keep.tile([P, PACK, HALF], BF16, name="raw2_first%d" % z) for z in range(2)]
        nc.sync.dma_start(out=first_halves[0][:], in_=core2_view[:, :, 0, :HALF])
        nc.sync.dma_start(out=t1_rows[:].rearrange("p (h r) -> p h r", h=N_TILES), in_=t1_view)
        nc.sync.dma_start(out=first_halves[1][:], in_=core2_view[:, :, 0, HALF:])
        for z in range(2):
            raw[(2, 0, z)] = first_halves[z][:]
        load_core3_quarter(0)
        load_core2_quarter(1)
        load_core3_quarter(1)
        raw3_last = keep.tile([P, 2 * PACK, 2, HALF], BF16, name="raw3_last")
        for z in range(2):
            rows = slice(PACK * z, PACK * (z + 1))
            nc.sync.dma_start(out=raw3_last[:, rows], in_=core3_view[:, rows, 2:4, :])
            for b in (2, 3):
                raw[(3, b, z)] = raw3_last[:, rows, b - 2, :]
        load_core2_quarter(2)
        load_core2_quarter(3)

        identity = keep.tile([P, P], F32, name="identity")
        make_identity(nc, identity[:])

        t1_grouped = keep.tile([P, N_TILES * K_PASS], BF16, name="t1_grouped", align_bytes=64)
        t1_codes = keep.tile([P, N_TILES * P], U32, name="t1_codes", align_bytes=64)
        t1_scales = keep.tile([P, N_TILES * P], U8, name="t1_scales", align_bytes=64)
        codes = {}
        scales = {}
        for core in (2, 3):
            codes[core] = keep.tile([P, N_QUARTERS, 2 * HALF], U32, name="codes%d" % core, align_bytes=64)
            scales[core] = keep.tile([P, N_QUARTERS, 2 * HALF], U8, name="scales%d" % core, align_bytes=64)
        t2_codes = keep.tile([P, N_QUARTERS, N_TILES, 2 * P], U32, name="t2_codes", align_bytes=64)
        t2_scales = keep.tile([P, N_QUARTERS, N_TILES, 2 * P], U8, name="t2_scales", align_bytes=64)

        def copy(engine, dst, src):
            if engine == "scalar":
                nc.scalar.copy(out=dst, in_=src)
            else:
                nc.vector.tensor_copy(out=dst, in_=src)

        grouped = {}

        def regroup(engine, core, n, z):
            if (core, n) not in grouped:
                grouped[(core, n)] = grouped_pool.tile([P, 2 * HALF * PACK], BF16, name="grouped", align_bytes=64)
            half = grouped[(core, n)][:, HALF * PACK * z : HALF * PACK * (z + 1)]
            dst = half.rearrange("p (c i t) -> p c t i", i=4, t=PACK)
            src = raw[(core, n, z)].rearrange("p t (c i) -> p c t i", i=4)
            split = GROUPS - SCALAR_GROUPS.get((core, n), 0)
            if engine == "scalar":
                copy(engine, dst[:, split:], src[:, split:])
            else:
                copy(engine, dst[:, :split], src[:, :split])

        def quantise(core, n, z):
            words = slice(HALF * z, HALF * (z + 1))
            nc.vector.quantize_mx(
                out=codes[core][:, n, words].bitcast(FP8X4),
                scales=scales[core][:, n, words],
                in_=grouped[(core, n)][:, HALF * PACK * z : HALF * PACK * (z + 1)],
            )

        def quantise_both(core, n):
            quantise(core, n, 0)
            quantise(core, n, 1)

        def prepare(core, n):
            regroup("vector", core, n, 0)
            regroup("vector", core, n, 1)
            quantise_both(core, n)

        t2_grouped = {}

        def step1(a, h):
            t2_grouped[(a, h)] = t2_pool.tile([P, 2, P, PACK], BF16, name="t2_grouped", align_bytes=64)
            rows = slice(h * P, (h + 1) * P)
            for g in range(2):
                bank = psum1.tile([P, PACK, P], F32, name="bank1", tag="bank1")
                for t in range(PACK):
                    cols = slice((PACK * g + t) * P, (PACK * g + t + 1) * P)
                    nc.tensor.matmul_mx(
                        out=bank[:, t, :],
                        lhsT=codes[2][:, a, cols].bitcast(FP8X4),
                        lhsT_scale=scales[2][:, a, cols],
                        rhs=t1_codes[:, rows].bitcast(FP8X4),
                        rhs_scale=t1_scales[:, rows],
                        start=True,
                        stop=True,
                    )
                engine = "vector" if (a == 2 and g == 1) else "scalar"
                copy(engine, t2_grouped[(a, h)][:, g], bank[:].rearrange("p t w -> p w t"))

        def quantise_t2(a, h):
            nc.vector.quantize_mx(
                out=t2_codes[:, a, h, :].bitcast(FP8X4),
                scales=t2_scales[:, a, h, :],
                in_=t2_grouped[(a, h)][:].rearrange("p g w t -> p (g w t)"),
            )

        stage = {}

        def store(dst_of_l, src_of_l):
            for l in range(4):
                nc.sync.dma_start(out=dst_of_l(l), in_=src_of_l(l))

        def step2(a, h, b):
            bank = psum2.tile([P, HALF], F32, name="bank2", tag="bank2")
            for g in range(2):
                nc.tensor.matmul_mx(
                    out=bank[:],
                    lhsT=t2_codes[:, a, h, g * P : (g + 1) * P].bitcast(FP8X4),
                    lhsT_scale=t2_scales[:, a, h, g * P : (g + 1) * P],
                    rhs=codes[3][:, b, g * HALF : (g + 1) * HALF].bitcast(FP8X4),
                    rhs_scale=scales[3][:, b, g * HALF : (g + 1) * HALF],
                    start=(g == 0),
                    stop=(g == 1),
                )
            i, o = b // 2, b % 2
            i1, o1 = a // 2, a % 2
            engine = "vector" if (a >= 2 and o == 1) else "scalar"
            if a < 2:
                key = ("both o1", h, i)
                if key not in stage:
                    stage[key] = stage_pool.tile([P, 2, 2, HALF], F32, name="stage", tag="stage")
                tile_s = stage[key]
                copy(engine, tile_s[:, o1, o, :], bank[:])
                if o1 == 1 and o == 1:
                    store(
                        lambda l: out_by_o1[4 * h + l, i1, i, :, :],
                        lambda l: tile_s[l:P:4].rearrange("p y o q -> p (y o q)"),
                    )
            else:
                key = ("both i", a, h)
                if key not in stage:
                    stage[key] = stage_pool.tile([P, 2, 2, HALF], F32, name="stage", tag="stage")
                tile_s = stage[key]
                copy(engine, tile_s[:, i, o, :], bank[:])
                very_last = a == N_QUARTERS - 1 and h == N_TILES - 1
                if very_last and o == 1:
                    store(
                        lambda l: out_by_i[4 * h + l, i1, o1, :, i, :],
                        lambda l: tile_s[l:P:4, i].rearrange("p o q -> p (o q)"),
                    )
                elif b == N_QUARTERS - 1:
                    store(
                        lambda l: out_by_i[4 * h + l, i1, o1, :, :, :],
                        lambda l: tile_s[l:P:4].rearrange("p i o q -> p i (o q)"),
                    )

        tiles = range(N_TILES)

        regroup("scalar", 2, 0, 0)
        regroup("vector", 2, 0, 0)
        quantise(2, 0, 0)

        t1_words = t1_rows[:].bitcast(F32).rearrange("p (h w u) -> p h u w", h=N_TILES, u=2)
        t1_grouped_words = t1_grouped[:].bitcast(F32).rearrange("p (h o l u) -> p h o l u", h=N_TILES, o=32, l=4, u=2)
        for h in tiles:
            planes = psum1.tile([P, 2, P], F32, name="planes", tag="bank1")
            for u in range(2):
                nc.tensor.transpose(planes[:, u, :], t1_words[:, h, u, :], identity[:])
            copy("scalar", t1_grouped_words[:, h], planes[:].rearrange("p u (l o) -> p o l u", l=4))

        regroup("scalar", 2, 0, 1)
        regroup("vector", 2, 0, 1)
        nc.vector.quantize_mx(out=t1_codes[:].bitcast(FP8X4), scales=t1_scales[:], in_=t1_grouped[:])
        quantise(2, 0, 1)
        regroup("scalar", 3, 0, 0)
        regroup("scalar", 3, 0, 1)

        for h in tiles:
            step1(0, h)
        prepare(3, 0)
        quantise_t2(0, 0)
        regroup("vector", 2, 1, 0)
        quantise_t2(0, 1)
        regroup("vector", 2, 1, 1)
        quantise_t2(0, 2)
        quantise_t2(0, 3)
        quantise_both(2, 1)
        for h in tiles:
            step2(0, h, 0)

        for h in tiles:
            step1(1, h)
        prepare(3, 1)
        quantise_t2(1, 0)
        quantise_t2(1, 1)
        regroup("vector", 3, 2, 0)
        quantise_t2(1, 2)
        quantise_t2(1, 3)
        regroup("vector", 3, 2, 1)
        quantise_both(3, 2)
        for h in tiles:
            step2(1, h, 0)

        for h in tiles:
            step2(0, h, 1)
            step2(1, h, 1)
        prepare(3, 3)
        for h in tiles:
            step2(0, h, 2)
            step2(1, h, 2)
        prepare(2, 2)
        prepare(2, 3)
        for h in tiles:
            step2(0, h, 3)
            step2(1, h, 3)
            step1(2, h)
            quantise_t2(2, h)
        copied = []
        for a in (2, 3):
            for h in tiles:
                for b in range(N_QUARTERS):
                    step2(a, h, b)
                    if b == 1 and copied:
                        quantise_t2(3, copied.pop())
                if a == 2:
                    step1(3, h)
                    copied.append(h)
